import numpy as np
import ml_dtypes

BF16 = ml_dtypes.bfloat16


def bf(x):
    return np.asarray(x, np.float32).astype(BF16)


def f32(x):
    return np.asarray(x, np.float32)


def f64(x):
    return np.asarray(x).astype(np.float64)


def striped(idx):
    return np.tile(idx.reshape(-1, 16).T, (8, 1))


D, S, F, N = 128, 2048, 512, 1024
RES = 1.15 + 0.2


def setup_inputs():
    a = np.sqrt(3.0 / D)
    return {"table": bf(0.8 * np.random.standard_normal((D, S))), "w_fc": bf(np.random.uniform(-a, a, (D, F))), "w_mp": bf(np.random.standard_normal((F, D)) / np.sqrt(F)), "offs": striped(np.random.permutation(np.tile(np.arange(S), 2))[:N])}


def reference(table, w_fc, w_mp, offs):
    idx = offs[:16].T.reshape(-1)
    t = f64(table)
    tn = t / np.sqrt(np.mean(t * t, axis=0, keepdims=True))
    xg = tn[:, idx]
    hid = np.square(np.maximum(f64(w_fc).T @ xg, 0.0))
    return RES * xg + f64(w_mp).T @ hid

@@ -1,0 +1,92 @@
+import math
+
+import concourse.mybir as mybir
+from concourse.masks import make_identity
+
+BF16 = mybir.dt.bfloat16
+F32 = mybir.dt.float32
+U16 = mybir.dt.uint16
+ACT = mybir.ActivationFunctionType
+
+P = 128
+WORDS = 2048
+HIDDEN = 512
+TOKENS = 1024
+BANK = 512
+WORD_CHUNKS = WORDS // BANK
+HIDDEN_BLOCKS = HIDDEN // P
+PIECES = TOKENS // BANK
+PIECE_COLS = BANK // 16
+RES = 1.35
+
+FLOPS = 4 * P * HIDDEN * TOKENS
+
+
+def tile_nanochatminilm_kernel(tc, table, w_fc, w_mp, offs, out):
+    nc = tc.nc
+    with (
+        tc.tile_pool(name="held", bufs=1) as held,
+        tc.tile_pool(name="work", bufs=2) as work,
+        tc.psum_pool(name="banks", bufs=6) as banks,
+        tc.psum_pool(name="sums", bufs=2) as sums,
+    ):
+        raw = held.tile([P, WORDS], BF16, name="raw")
+        for c in range(WORD_CHUNKS):
+            cols = slice(c * BANK, (c + 1) * BANK)
+            queue = nc.sync if c % 2 == 0 else nc.scalar
+            queue.dma_start(raw[:, cols], table[:, cols])
+        offsets = held.tile([P, TOKENS // 16], U16, name="offsets")
+        nc.sync.dma_start(offsets[:], offs)
+        fc = held.tile([P, HIDDEN], BF16, name="fc")
+        nc.scalar.dma_start(fc[:], w_fc)
+        mp = held.tile([P, HIDDEN_BLOCKS, P], BF16, name="mp")
+        nc.sync.dma_start(mp[:], w_mp.rearrange("(b p) d -> p b d", p=P))
+
+        ones = held.tile([P, P], BF16, name="ones")
+        nc.vector.memset(ones[:], 1.0)
+        identity = held.tile([P, P], BF16, name="identity")
+        make_identity(nc, identity[:])
+
+        tn = held.tile([P, WORDS], BF16, name="tn")
+        for c in range(WORD_CHUNKS):
+            cols = slice(c * BANK, (c + 1) * BANK)
+            squares = work.tile([P, BANK], BF16, name="squares")
+            nc.vector.tensor_mul(squares[:], raw[:, cols], raw[:, cols])
+            sum_sq = banks.tile([P, BANK], F32, name="sum_sq", tag="bank")
+            nc.tensor.matmul(sum_sq[:], ones[:], squares[:], start=True, stop=True)
+            inv_rms = work.tile([P, BANK], F32, name="inv_rms")
+            nc.scalar.activation(inv_rms[:], sum_sq[:], ACT.Abs_reciprocal_sqrt, scale=1.0 / P)
+            nc.vector.tensor_mul(tn[:, cols], raw[:, cols], inv_rms[:])
+
+        looked_up = [
+            tn[:].indirect(offsets[:, i * PIECE_COLS : (i + 1) * PIECE_COLS]) for i in range(PIECES)
+        ]
+        hid = []
+        for i in range(PIECES):
+            hid_i = held.tile([P, HIDDEN_BLOCKS, BANK], BF16, name=f"hid{i}")
+            hid.append(hid_i)
+            for b in range(HIDDEN_BLOCKS):
+                proj = banks.tile([P, BANK], F32, name="proj", tag="bank")
+                nc.tensor.matmul(proj[:], fc[:, b * P : (b + 1) * P], looked_up[i], start=True, stop=True)
+                relu = work.tile([P, BANK], F32, name="relu")
+                nc.scalar.activation(relu[:], proj[:], ACT.Relu, scale=1.0 / math.sqrt(RES))
+                nc.vector.tensor_mul(hid_i[:, b, :], relu[:], relu[:])
+
+        acc = []
+        for i in range(PIECES):
+            acc_i = sums.tile([P, BANK], F32, name="acc")
+            acc.append(acc_i)
+            nc.tensor.matmul(acc_i[:], identity[:], looked_up[i], start=True, stop=False)
+
+        for i in range(PIECES):
+            for b in range(HIDDEN_BLOCKS):
+                nc.tensor.matmul(
+                    acc[i][:], mp[:, b, :], hid[i][:, b, :], start=False, stop=(b == HIDDEN_BLOCKS - 1)
+                )
+            result = work.tile([P, BANK], F32, name="result")
+            if i % 2 == 0:
+                nc.scalar.mul(result[:], acc[i][:], RES)
+            else:
+                nc.vector.tensor_scalar_mul(result[:], acc[i][:], RES)
+            queue = nc.sync if i % 2 == 0 else nc.scalar
+            queue.dma_start(out[:, i * BANK : (i + 1) * BANK], result[:])

@@ -18,6 +18,7 @@ HIDDEN_BLOCKS = HIDDEN // P
 PIECES = TOKENS // BANK
 PIECE_COLS = BANK // 16
 RES = 1.35
+WARM_UP = 4
 
 FLOPS = 4 * P * HIDDEN * TOKENS
 
@@ -42,10 +43,14 @@ def tile_nanochatminilm_kernel(tc, table, w_fc, w_mp, offs, out):
         mp = held.tile([P, HIDDEN_BLOCKS, P], BF16, name="mp")
         nc.sync.dma_start(mp[:], w_mp.rearrange("(b p) d -> p b d", p=P))
 
-        ones = held.tile([P, P], BF16, name="ones")
+        ones = held.tile([P, BANK], BF16, name="ones")
         nc.vector.memset(ones[:], 1.0)
         identity = held.tile([P, P], BF16, name="identity")
         make_identity(nc, identity[:])
+
+        idle_work = banks.tile([P, BANK], F32, name="idle_work", tag="bank")
+        for repeat in range(WARM_UP):
+            nc.tensor.matmul(idle_work[:], ones[:, :P], ones[:], start=True, stop=True)
 
         tn = held.tile([P, WORDS], BF16, name="tn")
         for c in range(WORD_CHUNKS):
@@ -53,10 +58,13 @@ def tile_nanochatminilm_kernel(tc, table, w_fc, w_mp, offs, out):
             squares = work.tile([P, BANK], BF16, name="squares")
             nc.vector.tensor_mul(squares[:], raw[:, cols], raw[:, cols])
             sum_sq = banks.tile([P, BANK], F32, name="sum_sq", tag="bank")
-            nc.tensor.matmul(sum_sq[:], ones[:], squares[:], start=True, stop=True)
+            nc.tensor.matmul(sum_sq[:], ones[:, :P], squares[:], start=True, stop=True)
             inv_rms = work.tile([P, BANK], F32, name="inv_rms")
             nc.scalar.activation(inv_rms[:], sum_sq[:], ACT.Abs_reciprocal_sqrt, scale=1.0 / P)
             nc.vector.tensor_mul(tn[:, cols], raw[:, cols], inv_rms[:])
+            if c < WORD_CHUNKS - 1:
+                idle_work = banks.tile([P, BANK], F32, name="idle_work", tag="bank")
+                nc.tensor.matmul(idle_work[:], ones[:, :P], tn[:, cols], start=True, stop=True)
 
         looked_up = [
             tn[:].indirect(offsets[:, i * PIECE_COLS : (i + 1) * PIECE_COLS]) for i in range(PIECES)

@@ -13,12 +13,14 @@ WORDS = 2048
 HIDDEN = 512
 TOKENS = 1024
 BANK = 512
-WORD_CHUNKS = WORDS // BANK
+LOADS = 4
+PSUM_BANKS = 8
+WORD_CHUNKS = PSUM_BANKS
+CHUNK = WORDS // WORD_CHUNKS
 HIDDEN_BLOCKS = HIDDEN // P
 PIECES = TOKENS // BANK
 PIECE_COLS = BANK // 16
 RES = 1.35
-WARM_UP = 4
 
 FLOPS = 4 * P * HIDDEN * TOKENS
 
@@ -28,13 +30,12 @@ def tile_nanochatminilm_kernel(tc, table, w_fc, w_mp, offs, out):
     with (
         tc.tile_pool(name="held", bufs=1) as held,
         tc.tile_pool(name="work", bufs=2) as work,
-        tc.psum_pool(name="banks", bufs=6) as banks,
-        tc.psum_pool(name="sums", bufs=2) as sums,
+        tc.psum_pool(name="psum", bufs=1) as psum,
     ):
         raw = held.tile([P, WORDS], BF16, name="raw")
-        for c in range(WORD_CHUNKS):
-            cols = slice(c * BANK, (c + 1) * BANK)
-            queue = nc.sync if c % 2 == 0 else nc.scalar
+        for q in range(LOADS):
+            cols = slice(q * WORDS // LOADS, (q + 1) * WORDS // LOADS)
+            queue = nc.sync if q % 2 == 0 else nc.scalar
             queue.dma_start(raw[:, cols], table[:, cols])
         offsets = held.tile([P, TOKENS // 16], U16, name="offsets")
         nc.sync.dma_start(offsets[:], offs)
@@ -43,28 +44,24 @@ def tile_nanochatminilm_kernel(tc, table, w_fc, w_mp, offs, out):
         mp = held.tile([P, HIDDEN_BLOCKS, P], BF16, name="mp")
         nc.sync.dma_start(mp[:], w_mp.rearrange("(b p) d -> p b d", p=P))
 
-        ones = held.tile([P, BANK], BF16, name="ones")
+        bank = [psum.tile([P, BANK], F32, name=f"bank{n}") for n in range(PSUM_BANKS)]
+
+        ones = held.tile([P, P], BF16, name="ones")
         nc.vector.memset(ones[:], 1.0)
         identity = held.tile([P, P], BF16, name="identity")
         make_identity(nc, identity[:])
 
-        idle_work = banks.tile([P, BANK], F32, name="idle_work", tag="bank")
-        for repeat in range(WARM_UP):
-            nc.tensor.matmul(idle_work[:], ones[:, :P], ones[:], start=True, stop=True)
-
         tn = held.tile([P, WORDS], BF16, name="tn")
         for c in range(WORD_CHUNKS):
-            cols = slice(c * BANK, (c + 1) * BANK)
-            squares = work.tile([P, BANK], BF16, name="squares")
+            cols = slice(c * CHUNK, (c + 1) * CHUNK)
+            squares = work.tile([P, CHUNK], BF16, name="squares", bufs=WORD_CHUNKS)
             nc.vector.tensor_mul(squares[:], raw[:, cols], raw[:, cols])
-            sum_sq = banks.tile([P, BANK], F32, name="sum_sq", tag="bank")
-            nc.tensor.matmul(sum_sq[:], ones[:, :P], squares[:], start=True, stop=True)
-            inv_rms = work.tile([P, BANK], F32, name="inv_rms")
-            nc.scalar.activation(inv_rms[:], sum_sq[:], ACT.Abs_reciprocal_sqrt, scale=1.0 / P)
+            nc.tensor.matmul(bank[c][:, :CHUNK], ones[:], squares[:], start=True, stop=True)
+        for c in range(WORD_CHUNKS):
+            cols = slice(c * CHUNK, (c + 1) * CHUNK)
+            inv_rms = work.tile([P, CHUNK], F32, name="inv_rms", bufs=WORD_CHUNKS)
+            nc.scalar.activation(inv_rms[:], bank[c][:, :CHUNK], ACT.Abs_reciprocal_sqrt, scale=1.0 / P)
             nc.vector.tensor_mul(tn[:, cols], raw[:, cols], inv_rms[:])
-            if c < WORD_CHUNKS - 1:
-                idle_work = banks.tile([P, BANK], F32, name="idle_work", tag="bank")
-                nc.tensor.matmul(idle_work[:], ones[:, :P], tn[:, cols], start=True, stop=True)
 
         looked_up = [
             tn[:].indirect(offsets[:, i * PIECE_COLS : (i + 1) * PIECE_COLS]) for i in range(PIECES)
@@ -74,17 +71,15 @@ def tile_nanochatminilm_kernel(tc, table, w_fc, w_mp, offs, out):
             hid_i = held.tile([P, HIDDEN_BLOCKS, BANK], BF16, name=f"hid{i}")
             hid.append(hid_i)
             for b in range(HIDDEN_BLOCKS):
-                proj = banks.tile([P, BANK], F32, name="proj", tag="bank")
+                proj = bank[i * HIDDEN_BLOCKS + b]
                 nc.tensor.matmul(proj[:], fc[:, b * P : (b + 1) * P], looked_up[i], start=True, stop=True)
-                relu = work.tile([P, BANK], F32, name="relu")
+                relu = work.tile([P, BANK], F32, name="relu", bufs=PIECES * HIDDEN_BLOCKS)
                 nc.scalar.activation(relu[:], proj[:], ACT.Relu, scale=1.0 / math.sqrt(RES))
                 nc.vector.tensor_mul(hid_i[:, b, :], relu[:], relu[:])
 
-        acc = []
+        acc = bank[:PIECES]
         for i in range(PIECES):
-            acc_i = sums.tile([P, BANK], F32, name="acc")
-            acc.append(acc_i)
-            nc.tensor.matmul(acc_i[:], identity[:], looked_up[i], start=True, stop=False)
+            nc.tensor.matmul(acc[i][:], identity[:], looked_up[i], start=True, stop=False)
 
         for i in range(PIECES):
             for b in range(HIDDEN_BLOCKS):

@@ -21,6 +21,8 @@ HIDDEN_BLOCKS = HIDDEN // P
 PIECES = TOKENS // BANK
 PIECE_COLS = BANK // 16
 RES = 1.35
+WARM_UP = 3
+KEEP_WARM = 8
 
 FLOPS = 4 * P * HIDDEN * TOKENS
 
@@ -46,22 +48,27 @@ def tile_nanochatminilm_kernel(tc, table, w_fc, w_mp, offs, out):
 
         bank = [psum.tile([P, BANK], F32, name=f"bank{n}") for n in range(PSUM_BANKS)]
 
-        ones = held.tile([P, P], BF16, name="ones")
+        ones = held.tile([P, BANK], BF16, name="ones")
         nc.vector.memset(ones[:], 1.0)
         identity = held.tile([P, P], BF16, name="identity")
         make_identity(nc, identity[:])
+
+        for repeat in range(WARM_UP):
+            nc.tensor.matmul(bank[0][:], ones[:, :P], ones[:], start=True, stop=True)
 
         tn = held.tile([P, WORDS], BF16, name="tn")
         for c in range(WORD_CHUNKS):
             cols = slice(c * CHUNK, (c + 1) * CHUNK)
             squares = work.tile([P, CHUNK], BF16, name="squares", bufs=WORD_CHUNKS)
             nc.vector.tensor_mul(squares[:], raw[:, cols], raw[:, cols])
-            nc.tensor.matmul(bank[c][:, :CHUNK], ones[:], squares[:], start=True, stop=True)
+            nc.tensor.matmul(bank[c][:, :CHUNK], ones[:, :P], squares[:], start=True, stop=True)
         for c in range(WORD_CHUNKS):
             cols = slice(c * CHUNK, (c + 1) * CHUNK)
             inv_rms = work.tile([P, CHUNK], F32, name="inv_rms", bufs=WORD_CHUNKS)
             nc.scalar.activation(inv_rms[:], bank[c][:, :CHUNK], ACT.Abs_reciprocal_sqrt, scale=1.0 / P)
             nc.vector.tensor_mul(tn[:, cols], raw[:, cols], inv_rms[:])
+        for repeat in range(KEEP_WARM):
+            nc.tensor.matmul(bank[0][:, :CHUNK], ones[:, :P], squares[:], start=True, stop=True)
 
         looked_up = [
             tn[:].indirect(offsets[:, i * PIECE_COLS : (i + 1) * PIECE_COLS]) for i in range(PIECES)

@@ -21,6 +21,7 @@ HIDDEN_BLOCKS = HIDDEN // P
 PIECES = TOKENS // BANK
 PIECE_COLS = BANK // 16
 RES = 1.35
+GROUP_WIDTHS = (512, 256, 256)
 WARM_UP = 3
 KEEP_WARM = 8
 
@@ -70,33 +71,31 @@ def tile_nanochatminilm_kernel(tc, table, w_fc, w_mp, offs, out):
         for repeat in range(KEEP_WARM):
             nc.tensor.matmul(bank[0][:, :CHUNK], ones[:, :P], squares[:], start=True, stop=True)
 
-        looked_up = [
-            tn[:].indirect(offsets[:, i * PIECE_COLS : (i + 1) * PIECE_COLS]) for i in range(PIECES)
-        ]
-        hid = []
+        hid = held.tile([P, HIDDEN_BLOCKS, TOKENS], BF16, name="hid")
         for i in range(PIECES):
-            hid_i = held.tile([P, HIDDEN_BLOCKS, BANK], BF16, name=f"hid{i}")
-            hid.append(hid_i)
+            cols = slice(i * BANK, (i + 1) * BANK)
+            looked_up = tn[:].indirect(offsets[:, i * PIECE_COLS : (i + 1) * PIECE_COLS])
             for b in range(HIDDEN_BLOCKS):
                 proj = bank[i * HIDDEN_BLOCKS + b]
-                nc.tensor.matmul(proj[:], fc[:, b * P : (b + 1) * P], looked_up[i], start=True, stop=True)
+                nc.tensor.matmul(proj[:], fc[:, b * P : (b + 1) * P], looked_up, start=True, stop=True)
                 relu = work.tile([P, BANK], F32, name="relu", bufs=PIECES * HIDDEN_BLOCKS)
                 nc.scalar.activation(relu[:], proj[:], ACT.Relu, scale=1.0 / math.sqrt(RES))
-                nc.vector.tensor_mul(hid_i[:, b, :], relu[:], relu[:])
+                nc.vector.tensor_mul(hid[:, b, cols], relu[:], relu[:])
 
-        acc = bank[:PIECES]
-        for i in range(PIECES):
-            nc.tensor.matmul(acc[i][:], identity[:], looked_up[i], start=True, stop=False)
+        firsts = [sum(GROUP_WIDTHS[:g]) for g in range(len(GROUP_WIDTHS))]
+        for g, (first, width) in enumerate(zip(firsts, GROUP_WIDTHS)):
+            looked_up = tn[:].indirect(offsets[:, first // 16 : (first + width) // 16])
+            nc.tensor.matmul(bank[g][:, :width], identity[:], looked_up, start=True, stop=False)
 
-        for i in range(PIECES):
+        for g, (first, width) in enumerate(zip(firsts, GROUP_WIDTHS)):
+            cols = slice(first, first + width)
             for b in range(HIDDEN_BLOCKS):
                 nc.tensor.matmul(
-                    acc[i][:], mp[:, b, :], hid[i][:, b, :], start=False, stop=(b == HIDDEN_BLOCKS - 1)
+                    bank[g][:, :width], mp[:, b, :], hid[:, b, cols], start=False, stop=(b == HIDDEN_BLOCKS - 1)
                 )
-            result = work.tile([P, BANK], F32, name="result")
-            if i % 2 == 0:
-                nc.scalar.mul(result[:], acc[i][:], RES)
+            result = work.tile([P, width], F32, name="result", tag=f"result{g}", bufs=1)
+            if g < len(GROUP_WIDTHS) - 1:
+                nc.scalar.mul(result[:], bank[g][:, :width], RES)
             else:
-                nc.vector.tensor_scalar_mul(result[:], acc[i][:], RES)
-            queue = nc.sync if i % 2 == 0 else nc.scalar
-            queue.dma_start(out[:, i * BANK : (i + 1) * BANK], result[:])
+                nc.vector.tensor_scalar_mul(result[:], bank[g][:, :width], RES)
+            nc.sync.dma_start(out[:, cols], result[:])

@@ -22,6 +22,7 @@ PIECES = TOKENS // BANK
 PIECE_COLS = BANK // 16
 RES = 1.35
 GROUP_WIDTHS = (512, 256, 256)
+STORE_COLS = 256
 WARM_UP = 3
 KEEP_WARM = 8
 
@@ -93,9 +94,11 @@ def tile_nanochatminilm_kernel(tc, table, w_fc, w_mp, offs, out):
                 nc.tensor.matmul(
                     bank[g][:, :width], mp[:, b, :], hid[:, b, cols], start=False, stop=(b == HIDDEN_BLOCKS - 1)
                 )
-            result = work.tile([P, width], F32, name="result", tag=f"result{g}", bufs=1)
-            if g < len(GROUP_WIDTHS) - 1:
-                nc.scalar.mul(result[:], bank[g][:, :width], RES)
-            else:
-                nc.vector.tensor_scalar_mul(result[:], bank[g][:, :width], RES)
-            nc.sync.dma_start(out[:, cols], result[:])
+            for part in range(0, width, STORE_COLS):
+                in_bank = slice(part, part + STORE_COLS)
+                result = work.tile([P, STORE_COLS], F32, name="result", bufs=TOKENS // STORE_COLS)
+                if g < len(GROUP_WIDTHS) - 1:
+                    nc.scalar.mul(result[:], bank[g][:, in_bank], RES)
+                else:
+                    nc.vector.tensor_scalar_mul(result[:], bank[g][:, in_bank], RES)
+                nc.sync.dma_start(out[:, first + part : first + part + STORE_COLS], result[:])

@@ -7,6 +7,7 @@ BF16 = mybir.dt.bfloat16
 F32 = mybir.dt.float32
 U16 = mybir.dt.uint16
 ACT = mybir.ActivationFunctionType
+ALU = mybir.AluOpType
 
 P = 128
 WORDS = 2048
@@ -21,8 +22,9 @@ HIDDEN_BLOCKS = HIDDEN // P
 PIECES = TOKENS // BANK
 PIECE_COLS = BANK // 16
 RES = 1.35
-GROUP_WIDTHS = (512, 256, 256)
-STORE_COLS = 256
+GROUP = BANK // 2
+GROUPS_PER_PIECE = BANK // GROUP
+BANKS_PER_PIECE = HIDDEN_BLOCKS + GROUPS_PER_PIECE
 WARM_UP = 3
 KEEP_WARM = 8
 
@@ -73,32 +75,35 @@ def tile_nanochatminilm_kernel(tc, table, w_fc, w_mp, offs, out):
             nc.tensor.matmul(bank[0][:, :CHUNK], ones[:, :P], squares[:], start=True, stop=True)
 
         hid = held.tile([P, HIDDEN_BLOCKS, TOKENS], BF16, name="hid")
+        accumulators = []
         for i in range(PIECES):
             cols = slice(i * BANK, (i + 1) * BANK)
             looked_up = tn[:].indirect(offsets[:, i * PIECE_COLS : (i + 1) * PIECE_COLS])
             for b in range(HIDDEN_BLOCKS):
-                proj = bank[i * HIDDEN_BLOCKS + b]
+                proj = bank[(i * BANKS_PER_PIECE + b) % PSUM_BANKS]
                 nc.tensor.matmul(proj[:], fc[:, b * P : (b + 1) * P], looked_up, start=True, stop=True)
                 relu = work.tile([P, BANK], F32, name="relu", bufs=PIECES * HIDDEN_BLOCKS)
-                nc.scalar.activation(relu[:], proj[:], ACT.Relu, scale=1.0 / math.sqrt(RES))
+                if i == 0 and b == 0:
+                    nc.vector.tensor_scalar(relu[:], proj[:], 1.0 / math.sqrt(RES), 0.0, ALU.mult, ALU.max)
+                else:
+                    nc.scalar.activation(relu[:], proj[:], ACT.Relu, scale=1.0 / math.sqrt(RES))
                 nc.vector.tensor_mul(hid[:, b, cols], relu[:], relu[:])
+            for n in range(GROUPS_PER_PIECE):
+                first = i * BANK + n * GROUP
+                accumulator = bank[(i * BANKS_PER_PIECE + HIDDEN_BLOCKS + n) % PSUM_BANKS]
+                looked_up = tn[:].indirect(offsets[:, first // 16 : (first + GROUP) // 16])
+                nc.tensor.matmul(accumulator[:, :GROUP], identity[:], looked_up, start=True, stop=False)
+                accumulators.append(accumulator)
 
-        firsts = [sum(GROUP_WIDTHS[:g]) for g in range(len(GROUP_WIDTHS))]
-        for g, (first, width) in enumerate(zip(firsts, GROUP_WIDTHS)):
-            looked_up = tn[:].indirect(offsets[:, first // 16 : (first + width) // 16])
-            nc.tensor.matmul(bank[g][:, :width], identity[:], looked_up, start=True, stop=False)
-
-        for g, (first, width) in enumerate(zip(firsts, GROUP_WIDTHS)):
-            cols = slice(first, first + width)
+        for g, accumulator in enumerate(accumulators):
+            cols = slice(g * GROUP, (g + 1) * GROUP)
             for b in range(HIDDEN_BLOCKS):
                 nc.tensor.matmul(
-                    bank[g][:, :width], mp[:, b, :], hid[:, b, cols], start=False, stop=(b == HIDDEN_BLOCKS - 1)
+                    accumulator[:, :GROUP], mp[:, b, :], hid[:, b, cols], start=False, stop=(b == HIDDEN_BLOCKS - 1)
                 )
-            for part in range(0, width, STORE_COLS):
-                in_bank = slice(part, part + STORE_COLS)
-                result = work.tile([P, STORE_COLS], F32, name="result", bufs=TOKENS // STORE_COLS)
-                if g < len(GROUP_WIDTHS) - 1:
-                    nc.scalar.mul(result[:], bank[g][:, in_bank], RES)
-                else:
-                    nc.vector.tensor_scalar_mul(result[:], bank[g][:, in_bank], RES)
-                nc.sync.dma_start(out[:, first + part : first + part + STORE_COLS], result[:])
+            result = work.tile([P, GROUP], F32, name="result", bufs=len(accumulators))
+            if g < len(accumulators) - 1:
+                nc.scalar.mul(result[:], accumulator[:, :GROUP], RES)
+            else:
+                nc.vector.tensor_scalar_mul(result[:], accumulator[:, :GROUP], RES)
+            nc.sync.dma_start(out[:, cols], result[:])

@@ -25,10 +25,13 @@ RES = 1.35
 GROUP = BANK // 2
 GROUPS_PER_PIECE = BANK // GROUP
 BANKS_PER_PIECE = HIDDEN_BLOCKS + GROUPS_PER_PIECE
-WARM_UP = 3
-KEEP_WARM = 8
 
 FLOPS = 4 * P * HIDDEN * TOKENS
+
+
+def pieces_of(chunk, halved):
+    width = CHUNK // 2 if halved else CHUNK
+    return [(first, first + width) for first in range(chunk * CHUNK, (chunk + 1) * CHUNK, width)]
 
 
 def tile_nanochatminilm_kernel(tc, table, w_fc, w_mp, offs, out):
@@ -52,27 +55,26 @@ def tile_nanochatminilm_kernel(tc, table, w_fc, w_mp, offs, out):
 
         bank = [psum.tile([P, BANK], F32, name=f"bank{n}") for n in range(PSUM_BANKS)]
 
-        ones = held.tile([P, BANK], BF16, name="ones")
+        ones = held.tile([P, P], BF16, name="ones")
         nc.vector.memset(ones[:], 1.0)
         identity = held.tile([P, P], BF16, name="identity")
         make_identity(nc, identity[:])
 
-        for repeat in range(WARM_UP):
-            nc.tensor.matmul(bank[0][:], ones[:, :P], ones[:], start=True, stop=True)
-
         tn = held.tile([P, WORDS], BF16, name="tn")
+        squares = held.tile([P, WORDS], BF16, name="squares")
         for c in range(WORD_CHUNKS):
-            cols = slice(c * CHUNK, (c + 1) * CHUNK)
-            squares = work.tile([P, CHUNK], BF16, name="squares", bufs=WORD_CHUNKS)
-            nc.vector.tensor_mul(squares[:], raw[:, cols], raw[:, cols])
-            nc.tensor.matmul(bank[c][:, :CHUNK], ones[:, :P], squares[:], start=True, stop=True)
+            for first, last in pieces_of(c, halved=(c == 0)):
+                cols = slice(first, last)
+                nc.vector.tensor_mul(squares[:, cols], raw[:, cols], raw[:, cols])
+                in_bank = slice(first - c * CHUNK, last - c * CHUNK)
+                nc.tensor.matmul(bank[c][:, in_bank], ones[:], squares[:, cols], start=True, stop=True)
+        inv_rms = held.tile([P, WORDS], F32, name="inv_rms")
         for c in range(WORD_CHUNKS):
-            cols = slice(c * CHUNK, (c + 1) * CHUNK)
-            inv_rms = work.tile([P, CHUNK], F32, name="inv_rms", bufs=WORD_CHUNKS)
-            nc.scalar.activation(inv_rms[:], bank[c][:, :CHUNK], ACT.Abs_reciprocal_sqrt, scale=1.0 / P)
-            nc.vector.tensor_mul(tn[:, cols], raw[:, cols], inv_rms[:])
-        for repeat in range(KEEP_WARM):
-            nc.tensor.matmul(bank[0][:, :CHUNK], ones[:, :P], squares[:], start=True, stop=True)
+            for first, last in pieces_of(c, halved=(c == WORD_CHUNKS - 1)):
+                cols = slice(first, last)
+                in_bank = slice(first - c * CHUNK, last - c * CHUNK)
+                nc.scalar.activation(inv_rms[:, cols], bank[c][:, in_bank], ACT.Abs_reciprocal_sqrt, scale=1.0 / P)
+                nc.vector.tensor_mul(tn[:, cols], raw[:, cols], inv_rms[:, cols])
 
         hid = held.tile([P, HIDDEN_BLOCKS, TOKENS], BF16, name="hid")
         accumulators = []
@@ -97,13 +99,20 @@ def tile_nanochatminilm_kernel(tc, table, w_fc, w_mp, offs, out):
 
         for g, accumulator in enumerate(accumulators):
             cols = slice(g * GROUP, (g + 1) * GROUP)
-            for b in range(HIDDEN_BLOCKS):
+            block_order = list(range(HIDDEN_BLOCKS))
+            if g % GROUPS_PER_PIECE > 0:
+                block_order.reverse()
+            for n, b in enumerate(block_order):
                 nc.tensor.matmul(
-                    accumulator[:, :GROUP], mp[:, b, :], hid[:, b, cols], start=False, stop=(b == HIDDEN_BLOCKS - 1)
+                    accumulator[:, :GROUP], mp[:, b, :], hid[:, b, cols], start=False, stop=(n == HIDDEN_BLOCKS - 1)
                 )
-            result = work.tile([P, GROUP], F32, name="result", bufs=len(accumulators))
-            if g < len(accumulators) - 1:
-                nc.scalar.mul(result[:], accumulator[:, :GROUP], RES)
-            else:
-                nc.vector.tensor_scalar_mul(result[:], accumulator[:, :GROUP], RES)
-            nc.sync.dma_start(out[:, cols], result[:])
+            last = g == len(accumulators) - 1
+            width = GROUP // 2 if last else GROUP
+            for part in range(0, GROUP, width):
+                result = work.tile([P, width], F32, name="result", tag=f"result{g}", bufs=GROUP // width)
+                scaled = accumulator[:, part : part + width]
+                if last:
+                    nc.vector.tensor_scalar_mul(result[:], scaled, RES)
+                else:
+                    nc.scalar.mul(result[:], scaled, RES)
+                nc.sync.dma_start(out[:, g * GROUP + part : g * GROUP + part + width], result[:])

@@ -24,7 +24,6 @@ PIECE_COLS = BANK // 16
 RES = 1.35
 GROUP = BANK // 2
 GROUPS_PER_PIECE = BANK // GROUP
-BANKS_PER_PIECE = HIDDEN_BLOCKS + GROUPS_PER_PIECE
 
 FLOPS = 4 * P * HIDDEN * TOKENS
 
@@ -77,12 +76,11 @@ def tile_nanochatminilm_kernel(tc, table, w_fc, w_mp, offs, out):
                 nc.vector.tensor_mul(tn[:, cols], raw[:, cols], inv_rms[:, cols])
 
         hid = held.tile([P, HIDDEN_BLOCKS, TOKENS], BF16, name="hid")
-        accumulators = []
         for i in range(PIECES):
             cols = slice(i * BANK, (i + 1) * BANK)
             looked_up = tn[:].indirect(offsets[:, i * PIECE_COLS : (i + 1) * PIECE_COLS])
             for b in range(HIDDEN_BLOCKS):
-                proj = bank[(i * BANKS_PER_PIECE + b) % PSUM_BANKS]
+                proj = bank[i * HIDDEN_BLOCKS + b]
                 nc.tensor.matmul(proj[:], fc[:, b * P : (b + 1) * P], looked_up, start=True, stop=True)
                 relu = work.tile([P, BANK], F32, name="relu", bufs=PIECES * HIDDEN_BLOCKS)
                 if i == 0 and b == 0:
@@ -90,12 +88,11 @@ def tile_nanochatminilm_kernel(tc, table, w_fc, w_mp, offs, out):
                 else:
                     nc.scalar.activation(relu[:], proj[:], ACT.Relu, scale=1.0 / math.sqrt(RES))
                 nc.vector.tensor_mul(hid[:, b, cols], relu[:], relu[:])
-            for n in range(GROUPS_PER_PIECE):
-                first = i * BANK + n * GROUP
-                accumulator = bank[(i * BANKS_PER_PIECE + HIDDEN_BLOCKS + n) % PSUM_BANKS]
-                looked_up = tn[:].indirect(offsets[:, first // 16 : (first + GROUP) // 16])
-                nc.tensor.matmul(accumulator[:, :GROUP], identity[:], looked_up, start=True, stop=False)
-                accumulators.append(accumulator)
+
+        accumulators = bank[: TOKENS // GROUP]
+        for g, accumulator in enumerate(accumulators):
+            looked_up = tn[:].indirect(offsets[:, g * GROUP // 16 : (g + 1) * GROUP // 16])
+            nc.tensor.matmul(accumulator[:, :GROUP], identity[:], looked_up, start=True, stop=False)
 
         for g, accumulator in enumerate(accumulators):
             cols = slice(g * GROUP, (g + 1) * GROUP)

@@ -14,7 +14,7 @@ WORDS = 2048
 HIDDEN = 512
 TOKENS = 1024
 BANK = 512
-LOADS = 4
+LOAD_CHUNKS = (1, 2, 2, 3)
 PSUM_BANKS = 8
 WORD_CHUNKS = PSUM_BANKS
 CHUNK = WORDS // WORD_CHUNKS
@@ -41,8 +41,9 @@ def tile_nanochatminilm_kernel(tc, table, w_fc, w_mp, offs, out):
         tc.psum_pool(name="psum", bufs=1) as psum,
     ):
         raw = held.tile([P, WORDS], BF16, name="raw")
-        for q in range(LOADS):
-            cols = slice(q * WORDS // LOADS, (q + 1) * WORDS // LOADS)
+        for q, chunks in enumerate(LOAD_CHUNKS):
+            first = sum(LOAD_CHUNKS[:q]) * CHUNK
+            cols = slice(first, first + chunks * CHUNK)
             queue = nc.sync if q % 2 == 0 else nc.scalar
             queue.dma_start(raw[:, cols], table[:, cols])
         offsets = held.tile([P, TOKENS // 16], U16, name="offsets")

@@ -14,7 +14,7 @@ WORDS = 2048
 HIDDEN = 512
 TOKENS = 1024
 BANK = 512
-LOAD_CHUNKS = (1, 2, 2, 3)
+LOAD_CHUNKS = (1, 2, 3, 2)
 PSUM_BANKS = 8
 WORD_CHUNKS = PSUM_BANKS
 CHUNK = WORDS // WORD_CHUNKS
@@ -49,7 +49,7 @@ def tile_nanochatminilm_kernel(tc, table, w_fc, w_mp, offs, out):
         offsets = held.tile([P, TOKENS // 16], U16, name="offsets")
         nc.sync.dma_start(offsets[:], offs)
         fc = held.tile([P, HIDDEN], BF16, name="fc")
-        nc.scalar.dma_start(fc[:], w_fc)
+        nc.sync.dma_start(fc[:], w_fc)
         mp = held.tile([P, HIDDEN_BLOCKS, P], BF16, name="mp")
         nc.sync.dma_start(mp[:], w_mp.rearrange("(b p) d -> p b d", p=P))
 

import math

import concourse.mybir as mybir
from concourse.masks import make_identity

BF16 = mybir.dt.bfloat16
F32 = mybir.dt.float32
U16 = mybir.dt.uint16
ACT = mybir.ActivationFunctionType
ALU = mybir.AluOpType

P = 128
WORDS = 2048
HIDDEN = 512
TOKENS = 1024
BANK = 512
LOAD_CHUNKS = (1, 2, 3, 2)
PSUM_BANKS = 8
WORD_CHUNKS = PSUM_BANKS
CHUNK = WORDS // WORD_CHUNKS
HIDDEN_BLOCKS = HIDDEN // P
PIECES = TOKENS // BANK
PIECE_COLS = BANK // 16
RES = 1.35
GROUP = BANK // 2
GROUPS_PER_PIECE = BANK // GROUP

FLOPS = 4 * P * HIDDEN * TOKENS


def pieces_of(chunk, halved):
    width = CHUNK // 2 if halved else CHUNK
    return [(first, first + width) for first in range(chunk * CHUNK, (chunk + 1) * CHUNK, width)]


def tile_nanochatminilm_kernel(tc, table, w_fc, w_mp, offs, out):
    nc = tc.nc
    with (
        tc.tile_pool(name="held", bufs=1) as held,
        tc.tile_pool(name="work", bufs=2) as work,
        tc.psum_pool(name="psum", bufs=1) as psum,
    ):
        raw = held.tile([P, WORDS], BF16, name="raw")
        for q, chunks in enumerate(LOAD_CHUNKS):
            first = sum(LOAD_CHUNKS[:q]) * CHUNK
            cols = slice(first, first + chunks * CHUNK)
            queue = nc.sync if q % 2 == 0 else nc.scalar
            queue.dma_start(raw[:, cols], table[:, cols])
        offsets = held.tile([P, TOKENS // 16], U16, name="offsets")
        nc.sync.dma_start(offsets[:], offs)
        fc = held.tile([P, HIDDEN], BF16, name="fc")
        nc.sync.dma_start(fc[:], w_fc)
        mp = held.tile([P, HIDDEN_BLOCKS, P], BF16, name="mp")
        nc.sync.dma_start(mp[:], w_mp.rearrange("(b p) d -> p b d", p=P))

        bank = [psum.tile([P, BANK], F32, name=f"bank{n}") for n in range(PSUM_BANKS)]

        ones = held.tile([P, P], BF16, name="ones")
        nc.vector.memset(ones[:], 1.0)
        identity = held.tile([P, P], BF16, name="identity")
        make_identity(nc, identity[:])

        tn = held.tile([P, WORDS], BF16, name="tn")
        squares = held.tile([P, WORDS], BF16, name="squares")
        for c in range(WORD_CHUNKS):
            for first, last in pieces_of(c, halved=(c == 0)):
                cols = slice(first, last)
                nc.vector.tensor_mul(squares[:, cols], raw[:, cols], raw[:, cols])
                in_bank = slice(first - c * CHUNK, last - c * CHUNK)
                nc.tensor.matmul(bank[c][:, in_bank], ones[:], squares[:, cols], start=True, stop=True)
        inv_rms = held.tile([P, WORDS], F32, name="inv_rms")
        for c in range(WORD_CHUNKS):
            for first, last in pieces_of(c, halved=(c == WORD_CHUNKS - 1)):
                cols = slice(first, last)
                in_bank = slice(first - c * CHUNK, last - c * CHUNK)
                nc.scalar.activation(inv_rms[:, cols], bank[c][:, in_bank], ACT.Abs_reciprocal_sqrt, scale=1.0 / P)
                nc.vector.tensor_mul(tn[:, cols], raw[:, cols], inv_rms[:, cols])

        hid = held.tile([P, HIDDEN_BLOCKS, TOKENS], BF16, name="hid")
        for i in range(PIECES):
            cols = slice(i * BANK, (i + 1) * BANK)
            looked_up = tn[:].indirect(offsets[:, i * PIECE_COLS : (i + 1) * PIECE_COLS])
            for b in range(HIDDEN_BLOCKS):
                proj = bank[i * HIDDEN_BLOCKS + b]
                nc.tensor.matmul(proj[:], fc[:, b * P : (b + 1) * P], looked_up, start=True, stop=True)
                relu = work.tile([P, BANK], F32, name="relu", bufs=PIECES * HIDDEN_BLOCKS)
                if i == 0 and b == 0:
                    nc.vector.tensor_scalar(relu[:], proj[:], 1.0 / math.sqrt(RES), 0.0, ALU.mult, ALU.max)
                else:
                    nc.scalar.activation(relu[:], proj[:], ACT.Relu, scale=1.0 / math.sqrt(RES))
                nc.vector.tensor_mul(hid[:, b, cols], relu[:], relu[:])

        accumulators = bank[: TOKENS // GROUP]
        for g, accumulator in enumerate(accumulators):
            looked_up = tn[:].indirect(offsets[:, g * GROUP // 16 : (g + 1) * GROUP // 16])
            nc.tensor.matmul(accumulator[:, :GROUP], identity[:], looked_up, start=True, stop=False)

        for g, accumulator in enumerate(accumulators):
            cols = slice(g * GROUP, (g + 1) * GROUP)
            block_order = list(range(HIDDEN_BLOCKS))
            if g % GROUPS_PER_PIECE > 0:
                block_order.reverse()
            for n, b in enumerate(block_order):
                nc.tensor.matmul(
                    accumulator[:, :GROUP], mp[:, b, :], hid[:, b, cols], start=False, stop=(n == HIDDEN_BLOCKS - 1)
                )
            last = g == len(accumulators) - 1
            width = GROUP // 2 if last else GROUP
            for part in range(0, GROUP, width):
                result = work.tile([P, width], F32, name="result", tag=f"result{g}", bufs=GROUP // width)
                scaled = accumulator[:, part : part + width]
                if last:
                    nc.vector.tensor_scalar_mul(result[:], scaled, RES)
                else:
                    nc.scalar.mul(result[:], scaled, RES)
                nc.sync.dma_start(out[:, g * GROUP + part : g * GROUP + part + width], result[:])
